import numpy as np
import ml_dtypes


def mxq(x, axis, fmt="e4m3"):
    dtype, down = {"e4m3": (ml_dtypes.float8_e4m3fn, 7), "e5m2": (ml_dtypes.float8_e5m2, 14)}[fmt]
    v = np.moveaxis(np.asarray(x, np.float32).astype(ml_dtypes.bfloat16).astype(np.float64), axis, -1)
    blocks = v.reshape(v.shape[:-1] + (-1, 32))
    amax = np.abs(blocks).max(-1, keepdims=True)
    byte = np.maximum(np.where(amax > 0, np.frexp(amax)[1] - 1 + 127, 0) - down, 1)
    scale = np.exp2(byte - 127.0)
    codes = (blocks / scale).astype(np.float32).astype(dtype).astype(np.float64)
    return np.moveaxis((codes * scale).reshape(v.shape), -1, axis)


BF16 = ml_dtypes.bfloat16


def bf(x):
    return np.asarray(x, np.float32).astype(BF16)


def f64(x):
    return np.asarray(x).astype(np.float64)


B, C, H, W = 1, 512, 128, 128


def setup_inputs():
    a = np.random.standard_normal((B, C, 1, 1))
    shared = np.random.standard_normal((B, 1, H, W))
    z = np.random.standard_normal((B, C, H, W))
    return {"x": bf((z + a * shared) * 1.4 / np.sqrt(H * W))}


def reference(x):
    x = f64(x)
    nch = x.shape[1]
    X = x[0].reshape(nch, -1)
    Xq = mxq(X, 1, "e4m3")
    gram = Xq @ Xq.T
    return gram[None, None]

@@ -1,0 +1,170 @@
+from contextlib import ExitStack
+
+import concourse.mybir as mybir
+from concourse.masks import make_identity
+
+BF16 = mybir.dt.bfloat16
+F32 = mybir.dt.float32
+U32 = mybir.dt.uint32
+U8 = mybir.dt.uint8
+FP8X4 = mybir.dt.float8_e4m3fn_x4
+
+P = 128
+CHANNELS = 512
+PIXELS = 128 * 128
+BLOCKS = CHANNELS // P
+PACK = 4
+K_PASS = P * PACK
+PASSES = PIXELS // K_PASS
+HALVES = 2
+BANK_PASSES = 2
+BANK_WORDS = BANK_PASSES * HALVES * P
+PAIR_COLS = BANK_PASSES * CHANNELS
+
+RUN_PASSES = 4
+RUNS = PASSES // RUN_PASSES
+RUN_PAIRS = RUN_PASSES // BANK_PASSES
+RUN_PIXELS = RUN_PASSES * K_PASS
+LOADS_AHEAD = 2
+
+FLOPS = 2 * CHANNELS * CHANNELS * PIXELS
+
+
+def first_block_right(i):
+    return i + 1 if i > 0 else 0
+
+
+def tile_gram_kernel(tc, x, out):
+    nc = tc.nc
+    pixels = x.rearrange("b c h w -> (b c) (h w)")
+    gram = out.rearrange("a b i j -> (a b i) j")
+
+    with ExitStack() as ctx:
+        keep = ctx.enter_context(tc.tile_pool(name="keep", bufs=1))
+        loads = ctx.enter_context(tc.tile_pool(name="loads", bufs=BLOCKS * (LOADS_AHEAD + 1)))
+        stage = ctx.enter_context(tc.tile_pool(name="stage", bufs=2 * RUN_PAIRS))
+        results = ctx.enter_context(tc.tile_pool(name="results", bufs=1))
+        open_sums = ctx.enter_context(tc.psum_pool(name="open_sums", bufs=1))
+        banks = ctx.enter_context(tc.psum_pool(name="banks", bufs=5))
+        ctx.enter_context(tc.manual_schedule())
+
+        identity = keep.tile([P, P], F32)
+        make_identity(nc, identity[:])
+
+        codes = keep.tile([P, PASSES * CHANNELS], U32, align_bytes=64)
+        scales = keep.tile([P, PASSES * CHANNELS], U8, align_bytes=64)
+
+        x_tiles = {}
+
+        def load_run(r):
+            for b in range(BLOCKS):
+                x_sb = loads.tile([P, RUN_PIXELS], BF16)
+                nc.sync.dma_start(
+                    out=x_sb[:],
+                    in_=pixels[b * P : (b + 1) * P, r * RUN_PIXELS : (r + 1) * RUN_PIXELS],
+                )
+                x_tiles[(r, b)] = x_sb
+
+        def transpose_and_quantise_run(r):
+            grouped = [
+                stage.tile([P, PAIR_COLS * PACK], BF16, align_bytes=64, name="grouped")
+                for pair in range(RUN_PAIRS)
+            ]
+            for b in range(BLOCKS):
+                words = x_tiles[(r, b)][:].bitcast(F32)
+                for pair in range(RUN_PAIRS):
+                    bank = banks.tile([P, BANK_WORDS], F32, tag="bank")
+                    for s in range(BANK_PASSES * HALVES):
+                        first_word = pair * BANK_WORDS + s * P
+                        nc.tensor.transpose(
+                            bank[:, s * P : (s + 1) * P],
+                            words[:, first_word : first_word + P],
+                            identity[:],
+                        )
+                    side_by_side = (
+                        grouped[pair][:]
+                        .bitcast(F32)
+                        .rearrange("p (g c u) -> p g c u", g=BANK_PASSES, u=HALVES)
+                    )
+                    empties = nc.vector.tensor_copy if (b * RUN_PAIRS + pair) % 4 == 3 else nc.scalar.copy
+                    empties(
+                        out=side_by_side[:, :, b * P : (b + 1) * P, :],
+                        in_=bank[:].rearrange("p (g u c) -> p g c u", g=BANK_PASSES, u=HALVES),
+                    )
+            for pair in range(RUN_PAIRS):
+                first_col = (r * RUN_PAIRS + pair) * PAIR_COLS
+                nc.vector.quantize_mx(
+                    out=codes[:, first_col : first_col + PAIR_COLS].bitcast(FP8X4),
+                    scales=scales[:, first_col : first_col + PAIR_COLS],
+                    in_=grouped[pair][:],
+                )
+
+        def multiply(acc, g, row_block, first_block, last_block):
+            rows = slice(g * CHANNELS + row_block * P, g * CHANNELS + (row_block + 1) * P)
+            cols = slice(g * CHANNELS + first_block * P, g * CHANNELS + (last_block + 1) * P)
+            nc.tensor.matmul_mx(
+                out=acc[:],
+                lhsT=codes[:, rows].bitcast(FP8X4),
+                lhsT_scale=scales[:, rows],
+                rhs=codes[:, cols].bitcast(FP8X4),
+                rhs_scale=scales[:, cols],
+                start=(g == 0),
+                stop=(g == PASSES - 1),
+            )
+
+        right_sums = [
+            open_sums.tile([P, (BLOCKS - first_block_right(i)) * P], F32, name="right_sum%d" % i)
+            for i in range(BLOCKS - 1)
+        ]
+
+        def multiply_right_of_diagonal(r):
+            for g in range(r * RUN_PASSES, (r + 1) * RUN_PASSES):
+                for i in range(BLOCKS - 1):
+                    multiply(right_sums[i], g, i, first_block_right(i), BLOCKS - 1)
+
+        def multiply_diagonal_and_store(j):
+            diagonal_sum = banks.tile([P, P], F32, tag="bank")
+            for g in range(PASSES):
+                multiply(diagonal_sum, g, j, j, j)
+            diagonal = results.tile([P, P], F32, name="diagonal%d" % j)
+            nc.vector.tensor_copy(out=diagonal[:], in_=diagonal_sum[:])
+            nc.sync.dma_start(out=gram[j * P : (j + 1) * P, j * P : (j + 1) * P], in_=diagonal[:])
+
+        for r in range(LOADS_AHEAD):
+            load_run(r)
+        for r in range(RUNS):
+            if r + LOADS_AHEAD < RUNS:
+                load_run(r + LOADS_AHEAD)
+            transpose_and_quantise_run(r)
+            if r > 0:
+                multiply_right_of_diagonal(r - 1)
+        multiply_right_of_diagonal(RUNS - 1)
+
+        right = [
+            results.tile([P, (BLOCKS - first_block_right(i)) * P], F32, name="right%d" % i)
+            for i in range(BLOCKS - 1)
+        ]
+        for i in range(BLOCKS - 1):
+            empties = nc.scalar.copy if i == 0 else nc.vector.tensor_copy
+            empties(out=right[i][:], in_=right_sums[i][:])
+            nc.sync.dma_start(
+                out=gram[i * P : (i + 1) * P, first_block_right(i) * P : CHANNELS], in_=right[i][:]
+            )
+
+        multiply_diagonal_and_store(1)
+
+        for j in range(1, BLOCKS):
+            left_bank = banks.tile([P, j * P], F32, tag="bank")
+            for i in range(j):
+                first_col = (j - first_block_right(i)) * P
+                nc.tensor.transpose(
+                    left_bank[:, i * P : (i + 1) * P],
+                    right[i][:, first_col : first_col + P],
+                    identity[:],
+                )
+            left = results.tile([P, j * P], F32, name="left%d" % j)
+            nc.scalar.copy(out=left[:], in_=left_bank[:])
+            nc.sync.dma_start(out=gram[j * P : (j + 1) * P, 0 : j * P], in_=left[:])
+
+        for j in range(2, BLOCKS):
+            multiply_diagonal_and_store(j)

@@ -21,10 +21,14 @@ BANK_PASSES = 2
 BANK_WORDS = BANK_PASSES * HALVES * P
 PAIR_COLS = BANK_PASSES * CHANNELS
 
-RUN_PASSES = 4
+RUN_PASSES = 2
 RUNS = PASSES // RUN_PASSES
 RUN_PAIRS = RUN_PASSES // BANK_PASSES
-RUN_PIXELS = RUN_PASSES * K_PASS
+
+LOAD_PASSES = 4
+LOAD_PIXELS = LOAD_PASSES * K_PASS
+LOADS = PASSES // LOAD_PASSES
+LOAD_RUNS = LOAD_PASSES // RUN_PASSES
 LOADS_AHEAD = 2
 
 FLOPS = 2 * CHANNELS * CHANNELS * PIXELS
@@ -42,7 +46,7 @@ def tile_gram_kernel(tc, x, out):
     with ExitStack() as ctx:
         keep = ctx.enter_context(tc.tile_pool(name="keep", bufs=1))
         loads = ctx.enter_context(tc.tile_pool(name="loads", bufs=BLOCKS * (LOADS_AHEAD + 1)))
-        stage = ctx.enter_context(tc.tile_pool(name="stage", bufs=2 * RUN_PAIRS))
+        stage = ctx.enter_context(tc.tile_pool(name="stage", bufs=4))
         results = ctx.enter_context(tc.tile_pool(name="results", bufs=1))
         open_sums = ctx.enter_context(tc.psum_pool(name="open_sums", bufs=1))
         banks = ctx.enter_context(tc.psum_pool(name="banks", bufs=5))
@@ -56,26 +60,27 @@ def tile_gram_kernel(tc, x, out):
 
         x_tiles = {}
 
-        def load_run(r):
+        def load(n):
             for b in range(BLOCKS):
-                x_sb = loads.tile([P, RUN_PIXELS], BF16)
+                x_sb = loads.tile([P, LOAD_PIXELS], BF16)
                 nc.sync.dma_start(
                     out=x_sb[:],
-                    in_=pixels[b * P : (b + 1) * P, r * RUN_PIXELS : (r + 1) * RUN_PIXELS],
+                    in_=pixels[b * P : (b + 1) * P, n * LOAD_PIXELS : (n + 1) * LOAD_PIXELS],
                 )
-                x_tiles[(r, b)] = x_sb
+                x_tiles[(n, b)] = x_sb
 
         def transpose_and_quantise_run(r):
             grouped = [
                 stage.tile([P, PAIR_COLS * PACK], BF16, align_bytes=64, name="grouped")
                 for pair in range(RUN_PAIRS)
             ]
+            n, run_in_load = divmod(r, LOAD_RUNS)
             for b in range(BLOCKS):
-                words = x_tiles[(r, b)][:].bitcast(F32)
+                words = x_tiles[(n, b)][:].bitcast(F32)
                 for pair in range(RUN_PAIRS):
                     bank = banks.tile([P, BANK_WORDS], F32, tag="bank")
                     for s in range(BANK_PASSES * HALVES):
-                        first_word = pair * BANK_WORDS + s * P
+                        first_word = (run_in_load * RUN_PAIRS + pair) * BANK_WORDS + s * P
                         nc.tensor.transpose(
                             bank[:, s * P : (s + 1) * P],
                             words[:, first_word : first_word + P],
@@ -130,11 +135,11 @@ def tile_gram_kernel(tc, x, out):
             nc.vector.tensor_copy(out=diagonal[:], in_=diagonal_sum[:])
             nc.sync.dma_start(out=gram[j * P : (j + 1) * P, j * P : (j + 1) * P], in_=diagonal[:])
 
-        for r in range(LOADS_AHEAD):
-            load_run(r)
+        for n in range(LOADS_AHEAD):
+            load(n)
         for r in range(RUNS):
-            if r + LOADS_AHEAD < RUNS:
-                load_run(r + LOADS_AHEAD)
+            if r % LOAD_RUNS == 0 and r // LOAD_RUNS + LOADS_AHEAD < LOADS:
+                load(r // LOAD_RUNS + LOADS_AHEAD)
             transpose_and_quantise_run(r)
             if r > 0:
                 multiply_right_of_diagonal(r - 1)

@@ -19,23 +19,22 @@ PASSES = PIXELS // K_PASS
 HALVES = 2
 BANK_PASSES = 2
 BANK_WORDS = BANK_PASSES * HALVES * P
-PAIR_COLS = BANK_PASSES * CHANNELS
 
 RUN_PASSES = 2
 RUNS = PASSES // RUN_PASSES
 RUN_PAIRS = RUN_PASSES // BANK_PASSES
 
-LOAD_PASSES = 4
+LOAD_PASSES = 2
 LOAD_PIXELS = LOAD_PASSES * K_PASS
 LOADS = PASSES // LOAD_PASSES
 LOAD_RUNS = LOAD_PASSES // RUN_PASSES
-LOADS_AHEAD = 2
+LOADS_AHEAD = 4
 
 FLOPS = 2 * CHANNELS * CHANNELS * PIXELS
 
 
-def first_block_right(i):
-    return i + 1 if i > 0 else 0
+STREAMED_FROM = (0, 2, 2)
+DIAGONALS_AFTER = (1, 3)
 
 
 def tile_gram_kernel(tc, x, out):
@@ -71,7 +70,7 @@ def tile_gram_kernel(tc, x, out):
 
         def transpose_and_quantise_run(r):
             grouped = [
-                stage.tile([P, PAIR_COLS * PACK], BF16, align_bytes=64, name="grouped")
+                stage.tile([P, BANK_PASSES * CHANNELS * PACK], BF16, align_bytes=64, name="grouped")
                 for pair in range(RUN_PAIRS)
             ]
             n, run_in_load = divmod(r, LOAD_RUNS)
@@ -96,12 +95,14 @@ def tile_gram_kernel(tc, x, out):
                         out=side_by_side[:, :, b * P : (b + 1) * P, :],
                         in_=bank[:].rearrange("p (g u c) -> p g c u", g=BANK_PASSES, u=HALVES),
                     )
-            for pair in range(RUN_PAIRS):
-                first_col = (r * RUN_PAIRS + pair) * PAIR_COLS
+            for k in range(RUN_PASSES):
+                pair, pass_in_pair = divmod(k, BANK_PASSES)
+                first_col = (r * RUN_PASSES + k) * CHANNELS
+                first_value = pass_in_pair * CHANNELS * PACK
                 nc.vector.quantize_mx(
-                    out=codes[:, first_col : first_col + PAIR_COLS].bitcast(FP8X4),
-                    scales=scales[:, first_col : first_col + PAIR_COLS],
-                    in_=grouped[pair][:],
+                    out=codes[:, first_col : first_col + CHANNELS].bitcast(FP8X4),
+                    scales=scales[:, first_col : first_col + CHANNELS],
+                    in_=grouped[pair][:, first_value : first_value + CHANNELS * PACK],
                 )
 
         def multiply(acc, g, row_block, first_block, last_block):
@@ -117,15 +118,15 @@ def tile_gram_kernel(tc, x, out):
                 stop=(g == PASSES - 1),
             )
 
-        right_sums = [
-            open_sums.tile([P, (BLOCKS - first_block_right(i)) * P], F32, name="right_sum%d" % i)
-            for i in range(BLOCKS - 1)
+        streamed_sums = [
+            open_sums.tile([P, (BLOCKS - STREAMED_FROM[i]) * P], F32, name="streamed_sum%d" % i)
+            for i in range(len(STREAMED_FROM))
         ]
 
-        def multiply_right_of_diagonal(r):
+        def multiply_streamed(r):
             for g in range(r * RUN_PASSES, (r + 1) * RUN_PASSES):
-                for i in range(BLOCKS - 1):
-                    multiply(right_sums[i], g, i, first_block_right(i), BLOCKS - 1)
+                for i in range(len(STREAMED_FROM)):
+                    multiply(streamed_sums[i], g, i, STREAMED_FROM[i], BLOCKS - 1)
 
         def multiply_diagonal_and_store(j):
             diagonal_sum = banks.tile([P, P], F32, tag="bank")
@@ -142,34 +143,33 @@ def tile_gram_kernel(tc, x, out):
                 load(r // LOAD_RUNS + LOADS_AHEAD)
             transpose_and_quantise_run(r)
             if r > 0:
-                multiply_right_of_diagonal(r - 1)
-        multiply_right_of_diagonal(RUNS - 1)
+                multiply_streamed(r - 1)
+        multiply_streamed(RUNS - 1)
 
-        right = [
-            results.tile([P, (BLOCKS - first_block_right(i)) * P], F32, name="right%d" % i)
-            for i in range(BLOCKS - 1)
+        streamed = [
+            results.tile([P, (BLOCKS - STREAMED_FROM[i]) * P], F32, name="streamed%d" % i)
+            for i in range(len(STREAMED_FROM))
         ]
-        for i in range(BLOCKS - 1):
+        for i in range(len(STREAMED_FROM)):
             empties = nc.scalar.copy if i == 0 else nc.vector.tensor_copy
-            empties(out=right[i][:], in_=right_sums[i][:])
+            empties(out=streamed[i][:], in_=streamed_sums[i][:])
             nc.sync.dma_start(
-                out=gram[i * P : (i + 1) * P, first_block_right(i) * P : CHANNELS], in_=right[i][:]
+                out=gram[i * P : (i + 1) * P, STREAMED_FROM[i] * P : CHANNELS], in_=streamed[i][:]
             )
 
-        multiply_diagonal_and_store(1)
+        multiply_diagonal_and_store(DIAGONALS_AFTER[0])
 
         for j in range(1, BLOCKS):
             left_bank = banks.tile([P, j * P], F32, tag="bank")
             for i in range(j):
-                first_col = (j - first_block_right(i)) * P
+                first_col = (j - STREAMED_FROM[i]) * P
                 nc.tensor.transpose(
                     left_bank[:, i * P : (i + 1) * P],
-                    right[i][:, first_col : first_col + P],
+                    streamed[i][:, first_col : first_col + P],
                     identity[:],
                 )
             left = results.tile([P, j * P], F32, name="left%d" % j)
             nc.scalar.copy(out=left[:], in_=left_bank[:])
             nc.sync.dma_start(out=gram[j * P : (j + 1) * P, 0 : j * P], in_=left[:])
 
-        for j in range(2, BLOCKS):
-            multiply_diagonal_and_store(j)
+        multiply_diagonal_and_store(DIAGONALS_AFTER[1])

@@ -128,10 +128,11 @@ def tile_gram_kernel(tc, x, out):
                 for i in range(len(STREAMED_FROM)):
                     multiply(streamed_sums[i], g, i, STREAMED_FROM[i], BLOCKS - 1)
 
-        def multiply_diagonal_and_store(j):
-            diagonal_sum = banks.tile([P, P], F32, tag="bank")
-            for g in range(PASSES):
+        def multiply_diagonal(diagonal_sum, j, first_pass, end_pass):
+            for g in range(first_pass, end_pass):
                 multiply(diagonal_sum, g, j, j, j)
+
+        def store_diagonal(diagonal_sum, j):
             diagonal = results.tile([P, P], F32, name="diagonal%d" % j)
             nc.vector.tensor_copy(out=diagonal[:], in_=diagonal_sum[:])
             nc.sync.dma_start(out=gram[j * P : (j + 1) * P, j * P : (j + 1) * P], in_=diagonal[:])
@@ -144,7 +145,11 @@ def tile_gram_kernel(tc, x, out):
             transpose_and_quantise_run(r)
             if r > 0:
                 multiply_streamed(r - 1)
+        first, second = DIAGONALS_AFTER
+        first_sum = banks.tile([P, P], F32, tag="bank")
+        multiply_diagonal(first_sum, first, 0, PASSES - RUN_PASSES)
         multiply_streamed(RUNS - 1)
+        multiply_diagonal(first_sum, first, PASSES - RUN_PASSES, PASSES)
 
         streamed = [
             results.tile([P, (BLOCKS - STREAMED_FROM[i]) * P], F32, name="streamed%d" % i)
@@ -156,8 +161,10 @@ def tile_gram_kernel(tc, x, out):
             nc.sync.dma_start(
                 out=gram[i * P : (i + 1) * P, STREAMED_FROM[i] * P : CHANNELS], in_=streamed[i][:]
             )
+        store_diagonal(first_sum, first)
 
-        multiply_diagonal_and_store(DIAGONALS_AFTER[0])
+        second_sum = banks.tile([P, P], F32, tag="bank")
+        multiply_diagonal(second_sum, second, 0, PASSES // 2)
 
         for j in range(1, BLOCKS):
             left_bank = banks.tile([P, j * P], F32, tag="bank")
@@ -172,4 +179,5 @@ def tile_gram_kernel(tc, x, out):
             nc.scalar.copy(out=left[:], in_=left_bank[:])
             nc.sync.dma_start(out=gram[j * P : (j + 1) * P, 0 : j * P], in_=left[:])
 
-        multiply_diagonal_and_store(DIAGONALS_AFTER[1])
+        multiply_diagonal(second_sum, second, PASSES // 2, PASSES)
+        store_diagonal(second_sum, second)

@@ -20,15 +20,15 @@ HALVES = 2
 BANK_PASSES = 2
 BANK_WORDS = BANK_PASSES * HALVES * P
 
-RUN_PASSES = 2
-RUNS = PASSES // RUN_PASSES
-RUN_PAIRS = RUN_PASSES // BANK_PASSES
+PAIRS = PASSES // BANK_PASSES
+PAIR_PIXELS = BANK_PASSES * K_PASS
 
-LOAD_PASSES = 2
-LOAD_PIXELS = LOAD_PASSES * K_PASS
-LOADS = PASSES // LOAD_PASSES
-LOAD_RUNS = LOAD_PASSES // RUN_PASSES
-LOADS_AHEAD = 4
+RUN_BANKS = 4
+
+LOAD_PAIRS = (1, 1, 2, 2, 2, 2, 2, 2, 1, 1)
+assert sum(LOAD_PAIRS) == PAIRS
+LONG_LOADS_AHEAD = 3
+SHORT_LOADS = 2
 
 FLOPS = 2 * CHANNELS * CHANNELS * PIXELS
 
@@ -44,8 +44,9 @@ def tile_gram_kernel(tc, x, out):
 
     with ExitStack() as ctx:
         keep = ctx.enter_context(tc.tile_pool(name="keep", bufs=1))
-        loads = ctx.enter_context(tc.tile_pool(name="loads", bufs=BLOCKS * (LOADS_AHEAD + 1)))
-        stage = ctx.enter_context(tc.tile_pool(name="stage", bufs=4))
+        short_loads = ctx.enter_context(tc.tile_pool(name="short_loads", bufs=BLOCKS * SHORT_LOADS))
+        long_loads = ctx.enter_context(tc.tile_pool(name="long_loads", bufs=BLOCKS * LONG_LOADS_AHEAD))
+        stage = ctx.enter_context(tc.tile_pool(name="stage", bufs=6))
         results = ctx.enter_context(tc.tile_pool(name="results", bufs=1))
         open_sums = ctx.enter_context(tc.psum_pool(name="open_sums", bufs=1))
         banks = ctx.enter_context(tc.psum_pool(name="banks", bufs=5))
@@ -57,48 +58,52 @@ def tile_gram_kernel(tc, x, out):
         codes = keep.tile([P, PASSES * CHANNELS], U32, align_bytes=64)
         scales = keep.tile([P, PASSES * CHANNELS], U8, align_bytes=64)
 
+        first_pair = [sum(LOAD_PAIRS[:n]) for n in range(len(LOAD_PAIRS))]
         x_tiles = {}
+        grouped = {}
 
         def load(n):
+            first_pixel = first_pair[n] * PAIR_PIXELS
+            width = LOAD_PAIRS[n] * PAIR_PIXELS
             for b in range(BLOCKS):
-                x_sb = loads.tile([P, LOAD_PIXELS], BF16)
+                if LOAD_PAIRS[n] == 1:
+                    x_sb = short_loads.tile([P, width], BF16, name="x_short")
+                else:
+                    x_sb = long_loads.tile([P, width], BF16, name="x_long")
                 nc.sync.dma_start(
-                    out=x_sb[:],
-                    in_=pixels[b * P : (b + 1) * P, n * LOAD_PIXELS : (n + 1) * LOAD_PIXELS],
+                    out=x_sb[:], in_=pixels[b * P : (b + 1) * P, first_pixel : first_pixel + width]
                 )
                 x_tiles[(n, b)] = x_sb
 
-        def transpose_and_quantise_run(r):
-            grouped = [
-                stage.tile([P, BANK_PASSES * CHANNELS * PACK], BF16, align_bytes=64, name="grouped")
-                for pair in range(RUN_PAIRS)
-            ]
-            n, run_in_load = divmod(r, LOAD_RUNS)
-            for b in range(BLOCKS):
+        def transpose_run(n, first_block, end_block):
+            filled = 0
+            for b in range(first_block, end_block):
                 words = x_tiles[(n, b)][:].bitcast(F32)
-                for pair in range(RUN_PAIRS):
+                for j in range(LOAD_PAIRS[n]):
                     bank = banks.tile([P, BANK_WORDS], F32, tag="bank")
                     for s in range(BANK_PASSES * HALVES):
-                        first_word = (run_in_load * RUN_PAIRS + pair) * BANK_WORDS + s * P
+                        first_word = j * BANK_WORDS + s * P
                         nc.tensor.transpose(
                             bank[:, s * P : (s + 1) * P],
                             words[:, first_word : first_word + P],
                             identity[:],
                         )
                     side_by_side = (
-                        grouped[pair][:]
+                        grouped[first_pair[n] + j][:]
                         .bitcast(F32)
                         .rearrange("p (g c u) -> p g c u", g=BANK_PASSES, u=HALVES)
                     )
-                    empties = nc.vector.tensor_copy if (b * RUN_PAIRS + pair) % 4 == 3 else nc.scalar.copy
+                    filled += 1
+                    empties = nc.vector.tensor_copy if filled == RUN_BANKS else nc.scalar.copy
                     empties(
                         out=side_by_side[:, :, b * P : (b + 1) * P, :],
                         in_=bank[:].rearrange("p (g u c) -> p g c u", g=BANK_PASSES, u=HALVES),
                     )
-            for k in range(RUN_PASSES):
-                pair, pass_in_pair = divmod(k, BANK_PASSES)
-                first_col = (r * RUN_PASSES + k) * CHANNELS
-                first_value = pass_in_pair * CHANNELS * PACK
+
+        def quantise(pair):
+            for k in range(BANK_PASSES):
+                first_col = (pair * BANK_PASSES + k) * CHANNELS
+                first_value = k * CHANNELS * PACK
                 nc.vector.quantize_mx(
                     out=codes[:, first_col : first_col + CHANNELS].bitcast(FP8X4),
                     scales=scales[:, first_col : first_col + CHANNELS],
@@ -123,8 +128,8 @@ def tile_gram_kernel(tc, x, out):
             for i in range(len(STREAMED_FROM))
         ]
 
-        def multiply_streamed(r):
-            for g in range(r * RUN_PASSES, (r + 1) * RUN_PASSES):
+        def multiply_streamed(passes):
+            for g in passes:
                 for i in range(len(STREAMED_FROM)):
                     multiply(streamed_sums[i], g, i, STREAMED_FROM[i], BLOCKS - 1)
 
@@ -137,19 +142,46 @@ def tile_gram_kernel(tc, x, out):
             nc.vector.tensor_copy(out=diagonal[:], in_=diagonal_sum[:])
             nc.sync.dma_start(out=gram[j * P : (j + 1) * P, j * P : (j + 1) * P], in_=diagonal[:])
 
-        for n in range(LOADS_AHEAD):
+        runs = []
+        for n in range(len(LOAD_PAIRS)):
+            run_blocks = RUN_BANKS // LOAD_PAIRS[n]
+            for first_block in range(0, BLOCKS, run_blocks):
+                whole = first_block + run_blocks == BLOCKS
+                first_pass = first_pair[n] * BANK_PASSES
+                completes = list(range(first_pass, first_pass + LOAD_PAIRS[n] * BANK_PASSES)) if whole else []
+                runs.append((n, first_block, first_block + run_blocks, completes))
+
+        loads_asked = SHORT_LOADS + LONG_LOADS_AHEAD
+        for n in range(loads_asked):
             load(n)
-        for r in range(RUNS):
-            if r % LOAD_RUNS == 0 and r // LOAD_RUNS + LOADS_AHEAD < LOADS:
-                load(r // LOAD_RUNS + LOADS_AHEAD)
-            transpose_and_quantise_run(r)
-            if r > 0:
-                multiply_streamed(r - 1)
+        in_hand = []
+        for k in range(len(runs)):
+            n, first_block, end_block, completes = runs[k]
+            if first_block == 0:
+                for j in range(LOAD_PAIRS[n]):
+                    grouped[first_pair[n] + j] = stage.tile(
+                        [P, BANK_PASSES * CHANNELS * PACK], BF16, align_bytes=64, name="grouped"
+                    )
+                if n > SHORT_LOADS and loads_asked < len(LOAD_PAIRS):
+                    load(loads_asked)
+                    loads_asked += 1
+            transpose_run(n, first_block, end_block)
+            for pair in range(first_pair[n], first_pair[n] + (LOAD_PAIRS[n] if completes else 0)):
+                quantise(pair)
+            gaps = 1
+            for later in runs[k:]:
+                if later[3]:
+                    break
+                gaps += 1
+            share = (len(in_hand) + gaps - 1) // gaps
+            multiply_streamed(in_hand[:share])
+            in_hand = in_hand[share:] + completes
+
         first, second = DIAGONALS_AFTER
         first_sum = banks.tile([P, P], F32, tag="bank")
-        multiply_diagonal(first_sum, first, 0, PASSES - RUN_PASSES)
-        multiply_streamed(RUNS - 1)
-        multiply_diagonal(first_sum, first, PASSES - RUN_PASSES, PASSES)
+        multiply_diagonal(first_sum, first, 0, in_hand[0])
+        multiply_streamed(in_hand)
+        multiply_diagonal(first_sum, first, in_hand[0], PASSES)
 
         streamed = [
             results.tile([P, (BLOCKS - STREAMED_FROM[i]) * P], F32, name="streamed%d" % i)

from contextlib import ExitStack

import concourse.mybir as mybir
from concourse.masks import make_identity

BF16 = mybir.dt.bfloat16
F32 = mybir.dt.float32
U32 = mybir.dt.uint32
U8 = mybir.dt.uint8
FP8X4 = mybir.dt.float8_e4m3fn_x4

P = 128
CHANNELS = 512
PIXELS = 128 * 128
BLOCKS = CHANNELS // P
PACK = 4
K_PASS = P * PACK
PASSES = PIXELS // K_PASS
HALVES = 2
BANK_PASSES = 2
BANK_WORDS = BANK_PASSES * HALVES * P

PAIRS = PASSES // BANK_PASSES
PAIR_PIXELS = BANK_PASSES * K_PASS

RUN_BANKS = 4

LOAD_PAIRS = (1, 1, 2, 2, 2, 2, 2, 2, 1, 1)
assert sum(LOAD_PAIRS) == PAIRS
LONG_LOADS_AHEAD = 3
SHORT_LOADS = 2

FLOPS = 2 * CHANNELS * CHANNELS * PIXELS


STREAMED_FROM = (0, 2, 2)
DIAGONALS_AFTER = (1, 3)


def tile_gram_kernel(tc, x, out):
    nc = tc.nc
    pixels = x.rearrange("b c h w -> (b c) (h w)")
    gram = out.rearrange("a b i j -> (a b i) j")

    with ExitStack() as ctx:
        keep = ctx.enter_context(tc.tile_pool(name="keep", bufs=1))
        short_loads = ctx.enter_context(tc.tile_pool(name="short_loads", bufs=BLOCKS * SHORT_LOADS))
        long_loads = ctx.enter_context(tc.tile_pool(name="long_loads", bufs=BLOCKS * LONG_LOADS_AHEAD))
        stage = ctx.enter_context(tc.tile_pool(name="stage", bufs=6))
        results = ctx.enter_context(tc.tile_pool(name="results", bufs=1))
        open_sums = ctx.enter_context(tc.psum_pool(name="open_sums", bufs=1))
        banks = ctx.enter_context(tc.psum_pool(name="banks", bufs=5))
        ctx.enter_context(tc.manual_schedule())

        identity = keep.tile([P, P], F32)
        make_identity(nc, identity[:])

        codes = keep.tile([P, PASSES * CHANNELS], U32, align_bytes=64)
        scales = keep.tile([P, PASSES * CHANNELS], U8, align_bytes=64)

        first_pair = [sum(LOAD_PAIRS[:n]) for n in range(len(LOAD_PAIRS))]
        x_tiles = {}
        grouped = {}

        def load(n):
            first_pixel = first_pair[n] * PAIR_PIXELS
            width = LOAD_PAIRS[n] * PAIR_PIXELS
            for b in range(BLOCKS):
                if LOAD_PAIRS[n] == 1:
                    x_sb = short_loads.tile([P, width], BF16, name="x_short")
                else:
                    x_sb = long_loads.tile([P, width], BF16, name="x_long")
                nc.sync.dma_start(
                    out=x_sb[:], in_=pixels[b * P : (b + 1) * P, first_pixel : first_pixel + width]
                )
                x_tiles[(n, b)] = x_sb

        def transpose_run(n, first_block, end_block):
            filled = 0
            for b in range(first_block, end_block):
                words = x_tiles[(n, b)][:].bitcast(F32)
                for j in range(LOAD_PAIRS[n]):
                    bank = banks.tile([P, BANK_WORDS], F32, tag="bank")
                    for s in range(BANK_PASSES * HALVES):
                        first_word = j * BANK_WORDS + s * P
                        nc.tensor.transpose(
                            bank[:, s * P : (s + 1) * P],
                            words[:, first_word : first_word + P],
                            identity[:],
                        )
                    side_by_side = (
                        grouped[first_pair[n] + j][:]
                        .bitcast(F32)
                        .rearrange("p (g c u) -> p g c u", g=BANK_PASSES, u=HALVES)
                    )
                    filled += 1
                    empties = nc.vector.tensor_copy if filled == RUN_BANKS else nc.scalar.copy
                    empties(
                        out=side_by_side[:, :, b * P : (b + 1) * P, :],
                        in_=bank[:].rearrange("p (g u c) -> p g c u", g=BANK_PASSES, u=HALVES),
                    )

        def quantise(pair):
            for k in range(BANK_PASSES):
                first_col = (pair * BANK_PASSES + k) * CHANNELS
                first_value = k * CHANNELS * PACK
                nc.vector.quantize_mx(
                    out=codes[:, first_col : first_col + CHANNELS].bitcast(FP8X4),
                    scales=scales[:, first_col : first_col + CHANNELS],
                    in_=grouped[pair][:, first_value : first_value + CHANNELS * PACK],
                )

        def multiply(acc, g, row_block, first_block, last_block):
            rows = slice(g * CHANNELS + row_block * P, g * CHANNELS + (row_block + 1) * P)
            cols = slice(g * CHANNELS + first_block * P, g * CHANNELS + (last_block + 1) * P)
            nc.tensor.matmul_mx(
                out=acc[:],
                lhsT=codes[:, rows].bitcast(FP8X4),
                lhsT_scale=scales[:, rows],
                rhs=codes[:, cols].bitcast(FP8X4),
                rhs_scale=scales[:, cols],
                start=(g == 0),
                stop=(g == PASSES - 1),
            )

        streamed_sums = [
            open_sums.tile([P, (BLOCKS - STREAMED_FROM[i]) * P], F32, name="streamed_sum%d" % i)
            for i in range(len(STREAMED_FROM))
        ]

        def multiply_streamed(passes):
            for g in passes:
                for i in range(len(STREAMED_FROM)):
                    multiply(streamed_sums[i], g, i, STREAMED_FROM[i], BLOCKS - 1)

        def multiply_diagonal(diagonal_sum, j, first_pass, end_pass):
            for g in range(first_pass, end_pass):
                multiply(diagonal_sum, g, j, j, j)

        def store_diagonal(diagonal_sum, j):
            diagonal = results.tile([P, P], F32, name="diagonal%d" % j)
            nc.vector.tensor_copy(out=diagonal[:], in_=diagonal_sum[:])
            nc.sync.dma_start(out=gram[j * P : (j + 1) * P, j * P : (j + 1) * P], in_=diagonal[:])

        runs = []
        for n in range(len(LOAD_PAIRS)):
            run_blocks = RUN_BANKS // LOAD_PAIRS[n]
            for first_block in range(0, BLOCKS, run_blocks):
                whole = first_block + run_blocks == BLOCKS
                first_pass = first_pair[n] * BANK_PASSES
                completes = list(range(first_pass, first_pass + LOAD_PAIRS[n] * BANK_PASSES)) if whole else []
                runs.append((n, first_block, first_block + run_blocks, completes))

        loads_asked = SHORT_LOADS + LONG_LOADS_AHEAD
        for n in range(loads_asked):
            load(n)
        in_hand = []
        for k in range(len(runs)):
            n, first_block, end_block, completes = runs[k]
            if first_block == 0:
                for j in range(LOAD_PAIRS[n]):
                    grouped[first_pair[n] + j] = stage.tile(
                        [P, BANK_PASSES * CHANNELS * PACK], BF16, align_bytes=64, name="grouped"
                    )
                if n > SHORT_LOADS and loads_asked < len(LOAD_PAIRS):
                    load(loads_asked)
                    loads_asked += 1
            transpose_run(n, first_block, end_block)
            for pair in range(first_pair[n], first_pair[n] + (LOAD_PAIRS[n] if completes else 0)):
                quantise(pair)
            gaps = 1
            for later in runs[k:]:
                if later[3]:
                    break
                gaps += 1
            share = (len(in_hand) + gaps - 1) // gaps
            multiply_streamed(in_hand[:share])
            in_hand = in_hand[share:] + completes

        first, second = DIAGONALS_AFTER
        first_sum = banks.tile([P, P], F32, tag="bank")
        multiply_diagonal(first_sum, first, 0, in_hand[0])
        multiply_streamed(in_hand)
        multiply_diagonal(first_sum, first, in_hand[0], PASSES)

        streamed = [
            results.tile([P, (BLOCKS - STREAMED_FROM[i]) * P], F32, name="streamed%d" % i)
            for i in range(len(STREAMED_FROM))
        ]
        for i in range(len(STREAMED_FROM)):
            empties = nc.scalar.copy if i == 0 else nc.vector.tensor_copy
            empties(out=streamed[i][:], in_=streamed_sums[i][:])
            nc.sync.dma_start(
                out=gram[i * P : (i + 1) * P, STREAMED_FROM[i] * P : CHANNELS], in_=streamed[i][:]
            )
        store_diagonal(first_sum, first)

        second_sum = banks.tile([P, P], F32, tag="bank")
        multiply_diagonal(second_sum, second, 0, PASSES // 2)

        for j in range(1, BLOCKS):
            left_bank = banks.tile([P, j * P], F32, tag="bank")
            for i in range(j):
                first_col = (j - STREAMED_FROM[i]) * P
                nc.tensor.transpose(
                    left_bank[:, i * P : (i + 1) * P],
                    streamed[i][:, first_col : first_col + P],
                    identity[:],
                )
            left = results.tile([P, j * P], F32, name="left%d" % j)
            nc.scalar.copy(out=left[:], in_=left_bank[:])
            nc.sync.dma_start(out=gram[j * P : (j + 1) * P, 0 : j * P], in_=left[:])

        multiply_diagonal(second_sum, second, PASSES // 2, PASSES)
        store_diagonal(second_sum, second)
